import numpy as np
import ml_dtypes

BF16 = ml_dtypes.bfloat16


def bf(x):
    return np.asarray(x, np.float32).astype(BF16)


def f32(x):
    return np.asarray(x, np.float32)


def f64(x):
    return np.asarray(x).astype(np.float64)


def striped(idx):
    return np.tile(idx.reshape(-1, 16).T, (8, 1))


C, S, N, KI, KT = 128, 256, 128, 1024, 768
A_IMG, A_TXT = 0.1, 0.15


def setup_inputs():
    return {
        "base": f32(np.random.standard_normal((C, S))),
        "emb": f32(np.random.standard_normal((C, N))),
        "img_feat": bf(np.random.standard_normal((KI, N))),
        "img_w": bf(np.random.standard_normal((KI, C)) / np.sqrt(KI)),
        "img_b": f32(np.random.standard_normal((C, 1))),
        "txt_feat": bf(np.random.standard_normal((KT, N))),
        "txt_w": bf(np.random.standard_normal((KT, C)) / np.sqrt(KT)),
        "txt_b": f32(np.random.standard_normal((C, 1))),
        "offs": striped(np.random.permutation(S)[:N]),
    }


def reference(base, emb, img_feat, img_w, img_b, txt_feat, txt_w, txt_b, offs):
    idx = offs[:16].T.reshape(-1)
    img_all = f64(img_w).T @ f64(img_feat) + f64(img_b)
    txt_all = f64(txt_w).T @ f64(txt_feat) + f64(txt_b)
    out = f64(base).copy()
    out[:, idx] = f64(emb) + (A_IMG * img_all + A_TXT * txt_all)
    return out

@@ -1,0 +1,75 @@
+import concourse.mybir as mybir
+
+F32, BF16, U16 = mybir.dt.float32, mybir.dt.bfloat16, mybir.dt.uint16
+MULT, ADD = mybir.AluOpType.mult, mybir.AluOpType.add
+
+P = 128
+S = 256
+N = 128
+KI, KT = 1024, 768
+A_IMG, A_TXT = 0.1, 0.15
+
+FLOPS = 2 * P * N * (KI + KT)
+
+
+def tile_hide_kernel(tc, base, emb, img_feat, img_w, img_b, txt_feat, txt_w, txt_b, offs, out):
+    nc = tc.nc
+    img_blocks, txt_blocks = KI // P, KT // P
+
+    with (
+        tc.tile_pool(name="held", bufs=1) as held,
+        tc.psum_pool(name="psum", bufs=1) as psum,
+    ):
+        offsets = held.tile([P, N // 16], U16, name="offsets")
+        nc.sync.dma_start(offsets[:], offs)
+
+        img_w_sb = held.tile([P, img_blocks * P], BF16, name="img_w_sb")
+        img_feat_sb = held.tile([P, img_blocks * N], BF16, name="img_feat_sb")
+        txt_w_sb = held.tile([P, txt_blocks * P], BF16, name="txt_w_sb")
+        txt_feat_sb = held.tile([P, txt_blocks * N], BF16, name="txt_feat_sb")
+        nc.sync.dma_start(img_w_sb[:], img_w.rearrange("(p b) c -> p (b c)", p=P))
+        nc.scalar.dma_start(img_feat_sb[:], img_feat.rearrange("(p b) j -> p (b j)", p=P))
+        nc.sync.dma_start(txt_w_sb[:], txt_w.rearrange("(p b) c -> p (b c)", p=P))
+        nc.scalar.dma_start(txt_feat_sb[:], txt_feat.rearrange("(p b) j -> p (b j)", p=P))
+
+        window = held.tile([P, S], F32, name="window")
+        emb_sb = held.tile([P, N], F32, name="emb_sb")
+        img_b_sb = held.tile([P, 1], F32, name="img_b_sb")
+        txt_b_sb = held.tile([P, 1], F32, name="txt_b_sb")
+        nc.sync.dma_start(window[:], base)
+        nc.scalar.dma_start(emb_sb[:], emb)
+        nc.sync.dma_start(img_b_sb[:], img_b)
+        nc.scalar.dma_start(txt_b_sb[:], txt_b)
+
+        img_b_scaled = held.tile([P, 1], F32, name="img_b_scaled")
+        bias_term = held.tile([P, 1], F32, name="bias_term")
+        nc.vector.tensor_scalar(img_b_scaled[:], img_b_sb[:], A_IMG, None, MULT)
+        nc.vector.scalar_tensor_tensor(bias_term[:], txt_b_sb[:], A_TXT, img_b_scaled[:], MULT, ADD)
+
+        img_ps = psum.tile([P, N], F32, name="img_ps")
+        for b in range(img_blocks):
+            nc.tensor.matmul(
+                img_ps[:],
+                img_w_sb[:, b * P : (b + 1) * P],
+                img_feat_sb[:, b * N : (b + 1) * N],
+                start=(b == 0),
+                stop=(b == img_blocks - 1),
+            )
+        txt_ps = psum.tile([P, N], F32, name="txt_ps")
+        for b in range(txt_blocks):
+            nc.tensor.matmul(
+                txt_ps[:],
+                txt_w_sb[:, b * P : (b + 1) * P],
+                txt_feat_sb[:, b * N : (b + 1) * N],
+                start=(b == 0),
+                stop=(b == txt_blocks - 1),
+            )
+
+        img_term = held.tile([P, N], F32, name="img_term")
+        term = held.tile([P, N], F32, name="term")
+        nc.vector.tensor_scalar(img_term[:], img_ps[:], A_IMG, bias_term[:], MULT, ADD)
+        nc.vector.scalar_tensor_tensor(term[:], txt_ps[:], A_TXT, img_term[:], MULT, ADD)
+
+        nc.vector.tensor_tensor(window[:].indirect(offsets[:]), emb_sb[:], term[:], ADD)
+
+        nc.sync.dma_start(out, window[:])

@@ -20,8 +20,10 @@ def tile_hide_kernel(tc, base, emb, img_feat, img_w, img_b, txt_feat, txt_w, txt
         tc.tile_pool(name="held", bufs=1) as held,
         tc.psum_pool(name="psum", bufs=1) as psum,
     ):
-        offsets = held.tile([P, N // 16], U16, name="offsets")
-        nc.sync.dma_start(offsets[:], offs)
+        img_b_sb = held.tile([P, 1], F32, name="img_b_sb")
+        txt_b_sb = held.tile([P, 1], F32, name="txt_b_sb")
+        nc.gpsimd.dma_start(img_b_sb[:], img_b)
+        nc.gpsimd.dma_start(txt_b_sb[:], txt_b)
 
         img_w_sb = held.tile([P, img_blocks * P], BF16, name="img_w_sb")
         img_feat_sb = held.tile([P, img_blocks * N], BF16, name="img_feat_sb")
@@ -32,14 +34,12 @@ def tile_hide_kernel(tc, base, emb, img_feat, img_w, img_b, txt_feat, txt_w, txt
         nc.sync.dma_start(txt_w_sb[:], txt_w.rearrange("(p b) c -> p (b c)", p=P))
         nc.scalar.dma_start(txt_feat_sb[:], txt_feat.rearrange("(p b) j -> p (b j)", p=P))
 
+        offsets = held.tile([P, N // 16], U16, name="offsets")
         window = held.tile([P, S], F32, name="window")
         emb_sb = held.tile([P, N], F32, name="emb_sb")
-        img_b_sb = held.tile([P, 1], F32, name="img_b_sb")
-        txt_b_sb = held.tile([P, 1], F32, name="txt_b_sb")
+        nc.sync.dma_start(offsets[:], offs)
         nc.sync.dma_start(window[:], base)
         nc.scalar.dma_start(emb_sb[:], emb)
-        nc.sync.dma_start(img_b_sb[:], img_b)
-        nc.scalar.dma_start(txt_b_sb[:], txt_b)
 
         img_b_scaled = held.tile([P, 1], F32, name="img_b_scaled")
         bias_term = held.tile([P, 1], F32, name="bias_term")

@@ -9,6 +9,9 @@ N = 128
 KI, KT = 1024, 768
 A_IMG, A_TXT = 0.1, 0.15
 
+WARM_COLUMNS = 512
+WARM_MATMULS = 4
+
 FLOPS = 2 * P * N * (KI + KT)
 
 
@@ -20,10 +23,16 @@ def tile_hide_kernel(tc, base, emb, img_feat, img_w, img_b, txt_feat, txt_w, txt
         tc.tile_pool(name="held", bufs=1) as held,
         tc.psum_pool(name="psum", bufs=1) as psum,
     ):
+        zeros = held.tile([P, WARM_COLUMNS], BF16, name="zeros")
+        warm_ps = psum.tile([P, WARM_COLUMNS], F32, name="warm_ps")
+        nc.vector.memset(zeros[:], 0.0)
+        for _ in range(WARM_MATMULS):
+            nc.tensor.matmul(warm_ps[:], zeros[:, 0:P], zeros[:], start=True, stop=True)
+
         img_b_sb = held.tile([P, 1], F32, name="img_b_sb")
         txt_b_sb = held.tile([P, 1], F32, name="txt_b_sb")
-        nc.gpsimd.dma_start(img_b_sb[:], img_b)
-        nc.gpsimd.dma_start(txt_b_sb[:], txt_b)
+        nc.sync.dma_start(img_b_sb[:], img_b)
+        nc.scalar.dma_start(txt_b_sb[:], txt_b)
 
         img_w_sb = held.tile([P, img_blocks * P], BF16, name="img_w_sb")
         img_feat_sb = held.tile([P, img_blocks * N], BF16, name="img_feat_sb")
@@ -39,7 +48,7 @@ def tile_hide_kernel(tc, base, emb, img_feat, img_w, img_b, txt_feat, txt_w, txt
         emb_sb = held.tile([P, N], F32, name="emb_sb")
         nc.sync.dma_start(offsets[:], offs)
         nc.sync.dma_start(window[:], base)
-        nc.scalar.dma_start(emb_sb[:], emb)
+        nc.gpsimd.dma_start(emb_sb[:], emb)
 
         img_b_scaled = held.tile([P, 1], F32, name="img_b_scaled")
         bias_term = held.tile([P, 1], F32, name="bias_term")

@@ -29,10 +29,10 @@ def tile_hide_kernel(tc, base, emb, img_feat, img_w, img_b, txt_feat, txt_w, txt
         for _ in range(WARM_MATMULS):
             nc.tensor.matmul(warm_ps[:], zeros[:, 0:P], zeros[:], start=True, stop=True)
 
-        img_b_sb = held.tile([P, 1], F32, name="img_b_sb")
-        txt_b_sb = held.tile([P, 1], F32, name="txt_b_sb")
-        nc.sync.dma_start(img_b_sb[:], img_b)
-        nc.scalar.dma_start(txt_b_sb[:], txt_b)
+        img_b_row = held.tile([1, P], F32, name="img_b_row")
+        txt_b_row = held.tile([1, P], F32, name="txt_b_row")
+        nc.sync.dma_start(img_b_row[:], img_b.rearrange("c one -> one c"))
+        nc.scalar.dma_start(txt_b_row[:], txt_b.rearrange("c one -> one c"))
 
         img_w_sb = held.tile([P, img_blocks * P], BF16, name="img_w_sb")
         img_feat_sb = held.tile([P, img_blocks * N], BF16, name="img_feat_sb")
@@ -50,33 +50,32 @@ def tile_hide_kernel(tc, base, emb, img_feat, img_w, img_b, txt_feat, txt_w, txt
         nc.sync.dma_start(window[:], base)
         nc.gpsimd.dma_start(emb_sb[:], emb)
 
-        img_b_scaled = held.tile([P, 1], F32, name="img_b_scaled")
-        bias_term = held.tile([P, 1], F32, name="bias_term")
-        nc.vector.tensor_scalar(img_b_scaled[:], img_b_sb[:], A_IMG, None, MULT)
-        nc.vector.scalar_tensor_tensor(bias_term[:], txt_b_sb[:], A_TXT, img_b_scaled[:], MULT, ADD)
-
+        ones_row = held.tile([1, N], F32, name="ones_row")
+        nc.vector.memset(ones_row[:], 1.0)
         img_ps = psum.tile([P, N], F32, name="img_ps")
+        txt_ps = psum.tile([P, N], F32, name="txt_ps")
+        nc.tensor.matmul(img_ps[:], img_b_row[:], ones_row[:], start=True, stop=False)
+        nc.tensor.matmul(txt_ps[:], txt_b_row[:], ones_row[:], start=True, stop=False)
         for b in range(img_blocks):
             nc.tensor.matmul(
                 img_ps[:],
                 img_w_sb[:, b * P : (b + 1) * P],
                 img_feat_sb[:, b * N : (b + 1) * N],
-                start=(b == 0),
+                start=False,
                 stop=(b == img_blocks - 1),
             )
-        txt_ps = psum.tile([P, N], F32, name="txt_ps")
         for b in range(txt_blocks):
             nc.tensor.matmul(
                 txt_ps[:],
                 txt_w_sb[:, b * P : (b + 1) * P],
                 txt_feat_sb[:, b * N : (b + 1) * N],
-                start=(b == 0),
+                start=False,
                 stop=(b == txt_blocks - 1),
             )
 
         img_term = held.tile([P, N], F32, name="img_term")
         term = held.tile([P, N], F32, name="term")
-        nc.vector.tensor_scalar(img_term[:], img_ps[:], A_IMG, bias_term[:], MULT, ADD)
+        nc.vector.tensor_scalar(img_term[:], img_ps[:], A_IMG, None, MULT)
         nc.vector.scalar_tensor_tensor(term[:], txt_ps[:], A_TXT, img_term[:], MULT, ADD)
 
         nc.vector.tensor_tensor(window[:].indirect(offsets[:]), emb_sb[:], term[:], ADD)

@@ -14,10 +14,31 @@ WARM_MATMULS = 4
 
 FLOPS = 2 * P * N * (KI + KT)
 
+LAST_BLOCKS = 2
+
+
+def load_blocks(queue, pool, dram, first, blocks, name):
+    loaded = pool.tile([P, blocks * P], BF16, name=name)
+    rows = dram[first * P : (first + blocks) * P, :]
+    queue.dma_start(loaded[:], rows.rearrange("(p b) c -> p (b c)", p=P))
+    return loaded
+
+
+def accumulate(nc, product, w_sb, feat_sb, blocks, opens, closes):
+    for b in range(blocks):
+        nc.tensor.matmul(
+            product[:],
+            w_sb[:, b * P : (b + 1) * P],
+            feat_sb[:, b * N : (b + 1) * N],
+            start=(opens and b == 0),
+            stop=(closes and b == blocks - 1),
+        )
+
 
 def tile_hide_kernel(tc, base, emb, img_feat, img_w, img_b, txt_feat, txt_w, txt_b, offs, out):
     nc = tc.nc
     img_blocks, txt_blocks = KI // P, KT // P
+    first_blocks = txt_blocks - LAST_BLOCKS
 
     with (
         tc.tile_pool(name="held", bufs=1) as held,
@@ -29,19 +50,17 @@ def tile_hide_kernel(tc, base, emb, img_feat, img_w, img_b, txt_feat, txt_w, txt
         for _ in range(WARM_MATMULS):
             nc.tensor.matmul(warm_ps[:], zeros[:, 0:P], zeros[:], start=True, stop=True)
 
-        img_b_row = held.tile([1, P], F32, name="img_b_row")
-        txt_b_row = held.tile([1, P], F32, name="txt_b_row")
-        nc.sync.dma_start(img_b_row[:], img_b.rearrange("c one -> one c"))
-        nc.scalar.dma_start(txt_b_row[:], txt_b.rearrange("c one -> one c"))
+        img_b_sb = held.tile([P, 1], F32, name="img_b_sb")
+        txt_b_sb = held.tile([P, 1], F32, name="txt_b_sb")
+        nc.sync.dma_start(img_b_sb[:], img_b)
+        nc.scalar.dma_start(txt_b_sb[:], txt_b)
 
-        img_w_sb = held.tile([P, img_blocks * P], BF16, name="img_w_sb")
-        img_feat_sb = held.tile([P, img_blocks * N], BF16, name="img_feat_sb")
-        txt_w_sb = held.tile([P, txt_blocks * P], BF16, name="txt_w_sb")
-        txt_feat_sb = held.tile([P, txt_blocks * N], BF16, name="txt_feat_sb")
-        nc.sync.dma_start(img_w_sb[:], img_w.rearrange("(p b) c -> p (b c)", p=P))
-        nc.scalar.dma_start(img_feat_sb[:], img_feat.rearrange("(p b) j -> p (b j)", p=P))
-        nc.sync.dma_start(txt_w_sb[:], txt_w.rearrange("(p b) c -> p (b c)", p=P))
-        nc.scalar.dma_start(txt_feat_sb[:], txt_feat.rearrange("(p b) j -> p (b j)", p=P))
+        img_w_sb = load_blocks(nc.sync, held, img_w, 0, img_blocks, "img_w_sb")
+        img_feat_sb = load_blocks(nc.scalar, held, img_feat, 0, img_blocks, "img_feat_sb")
+        txt_w_first = load_blocks(nc.sync, held, txt_w, 0, first_blocks, "txt_w_first")
+        txt_feat_first = load_blocks(nc.scalar, held, txt_feat, 0, first_blocks, "txt_feat_first")
+        txt_w_last = load_blocks(nc.sync, held, txt_w, first_blocks, LAST_BLOCKS, "txt_w_last")
+        txt_feat_last = load_blocks(nc.scalar, held, txt_feat, first_blocks, LAST_BLOCKS, "txt_feat_last")
 
         offsets = held.tile([P, N // 16], U16, name="offsets")
         window = held.tile([P, S], F32, name="window")
@@ -50,32 +69,20 @@ def tile_hide_kernel(tc, base, emb, img_feat, img_w, img_b, txt_feat, txt_w, txt
         nc.sync.dma_start(window[:], base)
         nc.gpsimd.dma_start(emb_sb[:], emb)
 
-        ones_row = held.tile([1, N], F32, name="ones_row")
-        nc.vector.memset(ones_row[:], 1.0)
+        img_b_scaled = held.tile([P, 1], F32, name="img_b_scaled")
+        bias_term = held.tile([P, 1], F32, name="bias_term")
+        nc.vector.tensor_scalar(img_b_scaled[:], img_b_sb[:], A_IMG, None, MULT)
+        nc.vector.scalar_tensor_tensor(bias_term[:], txt_b_sb[:], A_TXT, img_b_scaled[:], MULT, ADD)
+
         img_ps = psum.tile([P, N], F32, name="img_ps")
         txt_ps = psum.tile([P, N], F32, name="txt_ps")
-        nc.tensor.matmul(img_ps[:], img_b_row[:], ones_row[:], start=True, stop=False)
-        nc.tensor.matmul(txt_ps[:], txt_b_row[:], ones_row[:], start=True, stop=False)
-        for b in range(img_blocks):
-            nc.tensor.matmul(
-                img_ps[:],
-                img_w_sb[:, b * P : (b + 1) * P],
-                img_feat_sb[:, b * N : (b + 1) * N],
-                start=False,
-                stop=(b == img_blocks - 1),
-            )
-        for b in range(txt_blocks):
-            nc.tensor.matmul(
-                txt_ps[:],
-                txt_w_sb[:, b * P : (b + 1) * P],
-                txt_feat_sb[:, b * N : (b + 1) * N],
-                start=False,
-                stop=(b == txt_blocks - 1),
-            )
+        accumulate(nc, img_ps, img_w_sb, img_feat_sb, img_blocks, True, True)
+        accumulate(nc, txt_ps, txt_w_first, txt_feat_first, first_blocks, True, False)
+        accumulate(nc, txt_ps, txt_w_last, txt_feat_last, LAST_BLOCKS, False, True)
 
         img_term = held.tile([P, N], F32, name="img_term")
         term = held.tile([P, N], F32, name="term")
-        nc.vector.tensor_scalar(img_term[:], img_ps[:], A_IMG, None, MULT)
+        nc.vector.tensor_scalar(img_term[:], img_ps[:], A_IMG, bias_term[:], MULT, ADD)
         nc.vector.scalar_tensor_tensor(term[:], txt_ps[:], A_TXT, img_term[:], MULT, ADD)
 
         nc.vector.tensor_tensor(window[:].indirect(offsets[:]), emb_sb[:], term[:], ADD)

@@ -14,31 +14,10 @@ WARM_MATMULS = 4
 
 FLOPS = 2 * P * N * (KI + KT)
 
-LAST_BLOCKS = 2
-
-
-def load_blocks(queue, pool, dram, first, blocks, name):
-    loaded = pool.tile([P, blocks * P], BF16, name=name)
-    rows = dram[first * P : (first + blocks) * P, :]
-    queue.dma_start(loaded[:], rows.rearrange("(p b) c -> p (b c)", p=P))
-    return loaded
-
-
-def accumulate(nc, product, w_sb, feat_sb, blocks, opens, closes):
-    for b in range(blocks):
-        nc.tensor.matmul(
-            product[:],
-            w_sb[:, b * P : (b + 1) * P],
-            feat_sb[:, b * N : (b + 1) * N],
-            start=(opens and b == 0),
-            stop=(closes and b == blocks - 1),
-        )
-
 
 def tile_hide_kernel(tc, base, emb, img_feat, img_w, img_b, txt_feat, txt_w, txt_b, offs, out):
     nc = tc.nc
     img_blocks, txt_blocks = KI // P, KT // P
-    first_blocks = txt_blocks - LAST_BLOCKS
 
     with (
         tc.tile_pool(name="held", bufs=1) as held,
@@ -55,19 +34,21 @@ def tile_hide_kernel(tc, base, emb, img_feat, img_w, img_b, txt_feat, txt_w, txt
         nc.sync.dma_start(img_b_sb[:], img_b)
         nc.scalar.dma_start(txt_b_sb[:], txt_b)
 
-        img_w_sb = load_blocks(nc.sync, held, img_w, 0, img_blocks, "img_w_sb")
-        img_feat_sb = load_blocks(nc.scalar, held, img_feat, 0, img_blocks, "img_feat_sb")
-        txt_w_first = load_blocks(nc.sync, held, txt_w, 0, first_blocks, "txt_w_first")
-        txt_feat_first = load_blocks(nc.scalar, held, txt_feat, 0, first_blocks, "txt_feat_first")
-        txt_w_last = load_blocks(nc.sync, held, txt_w, first_blocks, LAST_BLOCKS, "txt_w_last")
-        txt_feat_last = load_blocks(nc.scalar, held, txt_feat, first_blocks, LAST_BLOCKS, "txt_feat_last")
+        img_w_sb = held.tile([P, img_blocks * P], BF16, name="img_w_sb")
+        img_feat_sb = held.tile([P, img_blocks * N], BF16, name="img_feat_sb")
+        txt_w_sb = held.tile([P, txt_blocks * P], BF16, name="txt_w_sb")
+        txt_feat_sb = held.tile([P, txt_blocks * N], BF16, name="txt_feat_sb")
+        nc.sync.dma_start(img_w_sb[:], img_w.rearrange("(p b) c -> p (b c)", p=P))
+        nc.scalar.dma_start(img_feat_sb[:], img_feat.rearrange("(p b) j -> p (b j)", p=P))
+        nc.sync.dma_start(txt_w_sb[:], txt_w.rearrange("(p b) c -> p (b c)", p=P))
+        nc.scalar.dma_start(txt_feat_sb[:], txt_feat.rearrange("(p b) j -> p (b j)", p=P))
 
         offsets = held.tile([P, N // 16], U16, name="offsets")
         window = held.tile([P, S], F32, name="window")
         emb_sb = held.tile([P, N], F32, name="emb_sb")
-        nc.sync.dma_start(offsets[:], offs)
         nc.sync.dma_start(window[:], base)
-        nc.gpsimd.dma_start(emb_sb[:], emb)
+        nc.scalar.dma_start(emb_sb[:], emb)
+        nc.sync.dma_start(offsets[:], offs)
 
         img_b_scaled = held.tile([P, 1], F32, name="img_b_scaled")
         bias_term = held.tile([P, 1], F32, name="bias_term")
@@ -75,10 +56,23 @@ def tile_hide_kernel(tc, base, emb, img_feat, img_w, img_b, txt_feat, txt_w, txt
         nc.vector.scalar_tensor_tensor(bias_term[:], txt_b_sb[:], A_TXT, img_b_scaled[:], MULT, ADD)
 
         img_ps = psum.tile([P, N], F32, name="img_ps")
+        for b in range(img_blocks):
+            nc.tensor.matmul(
+                img_ps[:],
+                img_w_sb[:, b * P : (b + 1) * P],
+                img_feat_sb[:, b * N : (b + 1) * N],
+                start=(b == 0),
+                stop=(b == img_blocks - 1),
+            )
         txt_ps = psum.tile([P, N], F32, name="txt_ps")
-        accumulate(nc, img_ps, img_w_sb, img_feat_sb, img_blocks, True, True)
-        accumulate(nc, txt_ps, txt_w_first, txt_feat_first, first_blocks, True, False)
-        accumulate(nc, txt_ps, txt_w_last, txt_feat_last, LAST_BLOCKS, False, True)
+        for b in range(txt_blocks):
+            nc.tensor.matmul(
+                txt_ps[:],
+                txt_w_sb[:, b * P : (b + 1) * P],
+                txt_feat_sb[:, b * N : (b + 1) * N],
+                start=(b == 0),
+                stop=(b == txt_blocks - 1),
+            )
 
         img_term = held.tile([P, N], F32, name="img_term")
         term = held.tile([P, N], F32, name="term")

import concourse.mybir as mybir

F32, BF16, U16 = mybir.dt.float32, mybir.dt.bfloat16, mybir.dt.uint16
MULT, ADD = mybir.AluOpType.mult, mybir.AluOpType.add

P = 128
S = 256
N = 128
KI, KT = 1024, 768
A_IMG, A_TXT = 0.1, 0.15

WARM_COLUMNS = 512
WARM_MATMULS = 4

FLOPS = 2 * P * N * (KI + KT)


def tile_hide_kernel(tc, base, emb, img_feat, img_w, img_b, txt_feat, txt_w, txt_b, offs, out):
    nc = tc.nc
    img_blocks, txt_blocks = KI // P, KT // P

    with (
        tc.tile_pool(name="held", bufs=1) as held,
        tc.psum_pool(name="psum", bufs=1) as psum,
    ):
        zeros = held.tile([P, WARM_COLUMNS], BF16, name="zeros")
        warm_ps = psum.tile([P, WARM_COLUMNS], F32, name="warm_ps")
        nc.vector.memset(zeros[:], 0.0)
        for _ in range(WARM_MATMULS):
            nc.tensor.matmul(warm_ps[:], zeros[:, 0:P], zeros[:], start=True, stop=True)

        img_b_sb = held.tile([P, 1], F32, name="img_b_sb")
        txt_b_sb = held.tile([P, 1], F32, name="txt_b_sb")
        nc.sync.dma_start(img_b_sb[:], img_b)
        nc.scalar.dma_start(txt_b_sb[:], txt_b)

        img_w_sb = held.tile([P, img_blocks * P], BF16, name="img_w_sb")
        img_feat_sb = held.tile([P, img_blocks * N], BF16, name="img_feat_sb")
        txt_w_sb = held.tile([P, txt_blocks * P], BF16, name="txt_w_sb")
        txt_feat_sb = held.tile([P, txt_blocks * N], BF16, name="txt_feat_sb")
        nc.sync.dma_start(img_w_sb[:], img_w.rearrange("(p b) c -> p (b c)", p=P))
        nc.scalar.dma_start(img_feat_sb[:], img_feat.rearrange("(p b) j -> p (b j)", p=P))
        nc.sync.dma_start(txt_w_sb[:], txt_w.rearrange("(p b) c -> p (b c)", p=P))
        nc.scalar.dma_start(txt_feat_sb[:], txt_feat.rearrange("(p b) j -> p (b j)", p=P))

        offsets = held.tile([P, N // 16], U16, name="offsets")
        window = held.tile([P, S], F32, name="window")
        emb_sb = held.tile([P, N], F32, name="emb_sb")
        nc.sync.dma_start(window[:], base)
        nc.scalar.dma_start(emb_sb[:], emb)
        nc.sync.dma_start(offsets[:], offs)

        img_b_scaled = held.tile([P, 1], F32, name="img_b_scaled")
        bias_term = held.tile([P, 1], F32, name="bias_term")
        nc.vector.tensor_scalar(img_b_scaled[:], img_b_sb[:], A_IMG, None, MULT)
        nc.vector.scalar_tensor_tensor(bias_term[:], txt_b_sb[:], A_TXT, img_b_scaled[:], MULT, ADD)

        img_ps = psum.tile([P, N], F32, name="img_ps")
        for b in range(img_blocks):
            nc.tensor.matmul(
                img_ps[:],
                img_w_sb[:, b * P : (b + 1) * P],
                img_feat_sb[:, b * N : (b + 1) * N],
                start=(b == 0),
                stop=(b == img_blocks - 1),
            )
        txt_ps = psum.tile([P, N], F32, name="txt_ps")
        for b in range(txt_blocks):
            nc.tensor.matmul(
                txt_ps[:],
                txt_w_sb[:, b * P : (b + 1) * P],
                txt_feat_sb[:, b * N : (b + 1) * N],
                start=(b == 0),
                stop=(b == txt_blocks - 1),
            )

        img_term = held.tile([P, N], F32, name="img_term")
        term = held.tile([P, N], F32, name="term")
        nc.vector.tensor_scalar(img_term[:], img_ps[:], A_IMG, bias_term[:], MULT, ADD)
        nc.vector.scalar_tensor_tensor(term[:], txt_ps[:], A_TXT, img_term[:], MULT, ADD)

        nc.vector.tensor_tensor(window[:].indirect(offsets[:]), emb_sb[:], term[:], ADD)

        nc.sync.dma_start(out, window[:])
